import numpy as np
import ml_dtypes


def mxq(x, axis, fmt="e4m3"):
    dtype, down = {"e4m3": (ml_dtypes.float8_e4m3fn, 7), "e5m2": (ml_dtypes.float8_e5m2, 14)}[fmt]
    v = np.moveaxis(np.asarray(x, np.float32).astype(ml_dtypes.bfloat16).astype(np.float64), axis, -1)
    blocks = v.reshape(v.shape[:-1] + (-1, 32))
    amax = np.abs(blocks).max(-1, keepdims=True)
    byte = np.maximum(np.where(amax > 0, np.frexp(amax)[1] - 1 + 127, 0) - down, 1)
    scale = np.exp2(byte - 127.0)
    codes = (blocks / scale).astype(np.float32).astype(dtype).astype(np.float64)
    return np.moveaxis((codes * scale).reshape(v.shape), -1, axis)


WIDE = False


def mx_kscale(k):
    if not WIDE:
        return np.ones(k)
    levels = np.array([10, -10, 5, -5, 0])
    a = np.random.permutation(np.resize(levels, k // 512 * 4)).reshape(k // 512, 4)
    idx = np.arange(k)
    return np.exp2(a[idx // 512, idx % 128 // 32])


BF16 = ml_dtypes.bfloat16


def bf(x):
    return np.asarray(x, np.float32).astype(BF16)


def f64(x):
    return np.asarray(x).astype(np.float64)


B, S, H, R = 16, 384, 512, 3
N = S // R


def setup_inputs():
    t = mx_kscale(H)
    return {"h": bf(np.random.standard_normal((B, N, R, H))),
            "s2t_W1_w": bf(np.random.standard_normal((H, H)) / np.sqrt(H) * t[:, None]),
            "s2t_W1_b": bf(np.random.standard_normal(H) * 0.3 * t),
            "s2t_W_w": bf(np.random.standard_normal((H, H)) * 2.0 / np.sqrt(H) / t[None, :])}


def reference(h, s2t_W1_w, s2t_W1_b, s2t_W_w):
    hf = f64(h)
    rows = hf.reshape(B * N * R, H)
    f = np.maximum((mxq(rows, 1, "e4m3") @ mxq(f64(s2t_W1_w), 1, "e4m3").T) + f64(s2t_W1_b), 0.0)
    z = (mxq(f, 1, "e4m3") @ mxq(f64(s2t_W_w), 1, "e4m3").T).reshape(B, N, R, H)
    e = np.exp(z - z.max(-2, keepdims=True))
    p = e / e.sum(-2, keepdims=True)
    return (p * hf).sum(-2)

@@ -1,0 +1,280 @@
+from contextlib import ExitStack
+
+import concourse.mybir as mybir
+from concourse.masks import make_identity
+
+F32 = mybir.dt.float32
+BF16 = mybir.dt.bfloat16
+U32 = mybir.dt.uint32
+U8 = mybir.dt.uint8
+FP8X4 = mybir.dt.float8_e4m3fn_x4
+ACT = mybir.ActivationFunctionType
+ALU = mybir.AluOpType
+
+P = 128
+PACK = 4
+HALVES = 2
+BATCHES = 16
+TOKENS = 3
+H = 512
+TOK = TOKENS * P
+
+TOKEN_SLICES = ((0, 256), (256, 128))
+
+LN_GROUP = 7
+LN_CEILING = 2.0**60
+
+FIRST_HALF = (0, 1)
+SECOND_HALF = (2, 3)
+
+FLOPS = 2 * 2 * BATCHES * TOK * H * H
+
+
+def tile_blocksa_pa_t_kernel(tc, h, s2t_W1_w, s2t_W1_b, s2t_W_w, out):
+    nc = tc.nc
+    with ExitStack() as ctx:
+        keep = ctx.enter_context(tc.tile_pool(name="keep", bufs=1))
+        setup = ctx.enter_context(tc.tile_pool(name="setup", bufs=1))
+        work = ctx.enter_context(tc.tile_pool(name="work", bufs=2))
+        psum_t = ctx.enter_context(tc.psum_pool(name="psum_t", bufs=2))
+        psum_f = ctx.enter_context(tc.psum_pool(name="psum_f", bufs=2))
+        psum_d = ctx.enter_context(tc.psum_pool(name="psum_d", bufs=3))
+        psum_g = ctx.enter_context(tc.psum_pool(name="psum_g", bufs=1))
+        ctx.enter_context(tc.manual_schedule())
+
+        w1_rows = setup.tile([P, PACK, H], BF16)
+        nc.sync.dma_start(
+            out=w1_rows[:].rearrange("p (u e) k -> p u (e k)", u=HALVES),
+            in_=s2t_W1_w.rearrange("(u p e) k -> p u (e k)", u=HALVES, e=2),
+        )
+        bias_rows = setup.tile([P, H], BF16)
+        nc.vector.memset(bias_rows[:], 0.0)
+        nc.sync.dma_start(out=bias_rows[0:1, :], in_=s2t_W1_b.rearrange("(o k) -> o k", o=1))
+        h_all = keep.tile([P, BATCHES, TOKENS, H], BF16)
+        nc.sync.dma_start(out=h_all[:, 0], in_=h[0])
+        w_rows = setup.tile([P, PACK, H], BF16)
+        nc.sync.dma_start(out=w_rows[:], in_=s2t_W_w.rearrange("(a p) k -> p a k", p=P))
+        for b in range(1, BATCHES):
+            nc.sync.dma_start(out=h_all[:, b], in_=h[b])
+
+        ident_f32 = keep.tile([P, P], F32)
+        make_identity(nc, ident_f32[:])
+        ident_bf16 = keep.tile([P, P], BF16)
+        nc.vector.tensor_copy(out=ident_bf16[:], in_=ident_f32[:])
+        neg_ident_bf16 = keep.tile([P, P], BF16)
+        nc.vector.tensor_scalar_mul(out=neg_ident_bf16[:], in0=ident_f32[:], scalar1=-1.0)
+
+        def transpose_rows(row_tiles):
+            bank = psum_t.tile([P, 2, HALVES, P], F32)
+            for a, rows in enumerate(row_tiles):
+                words = rows.bitcast(F32)
+                for u in range(HALVES):
+                    nc.tensor.transpose(out=bank[:, a, u, :], in_=words[:, u * P : (u + 1) * P], identity=ident_f32[:])
+            return bank
+
+        def group_views(bank, count, grouped):
+            grouped_words = grouped.rearrange("p r t -> p (r t)").bitcast(F32)
+            return (
+                grouped_words.rearrange("p (a r u) -> p a r u", a=count, u=HALVES),
+                bank[:, 0:count].rearrange("p a u r -> p a r u"),
+            )
+
+        def quantise(grouped, codes, scales, first, count):
+            cols = slice(first, first + count)
+            nc.vector.quantize_mx(
+                out=codes[:, cols].bitcast(FP8X4),
+                scales=scales[:, cols],
+                in_=grouped[:, cols, :].rearrange("p c t -> p (c t)"),
+            )
+
+        def group_weight(rows, name):
+            grouped = setup.tile([P, H, PACK], BF16, align_bytes=64, name=name + "_grouped")
+            for a in range(0, PACK, 2):
+                bank = transpose_rows([rows[:, a, :], rows[:, a + 1, :]])
+                dst, src = group_views(bank, 2, grouped[:, a * P : (a + 2) * P, :])
+                nc.scalar.copy(out=dst, in_=src)
+            codes = keep.tile([P, H], U32, align_bytes=64, name=name + "_codes")
+            scales = keep.tile([P, H], U8, align_bytes=64, name=name + "_scales")
+            return grouped, codes, scales
+
+        h_banks, h_grouped, h_codes, h_scales = {}, {}, {}, {}
+        f_acc, f_planes, f_grouped, f_codes, f_scales = {}, {}, {}, {}, {}
+        z_diff, h1_minus_h0, t01, e_to_2 = {}, {}, {}, {}
+        share2 = keep.tile([P, BATCHES, H], F32)
+        pair = keep.tile([P, BATCHES, H], F32)
+        rest = keep.tile([P, BATCHES, H], F32)
+
+        def transpose_h(b):
+            h_banks[b] = (transpose_rows([h_all[:, b, 0, :], h_all[:, b, 1, :]]), transpose_rows([h_all[:, b, 2, :]]))
+            h_grouped[b] = work.tile([P, TOK, PACK], BF16, align_bytes=64, name="h_grouped")
+
+        def group_h_tokens_01(b):
+            dst, src = group_views(h_banks[b][0], 2, h_grouped[b][:, 0 : 2 * P, :])
+            nc.scalar.copy(out=dst, in_=src)
+
+        def group_h_token_2(b):
+            dst, src = group_views(h_banks[b][1], 1, h_grouped[b][:, 2 * P : 3 * P, :])
+            nc.vector.tensor_copy(out=dst, in_=src)
+
+        def quantise_h(b):
+            h_codes[b] = work.tile([P, TOK], U32, align_bytes=64, name="h_codes")
+            h_scales[b] = work.tile([P, TOK], U8, align_bytes=64, name="h_scales")
+            for first, count in TOKEN_SLICES:
+                quantise(h_grouped[b], h_codes[b], h_scales[b], first, count)
+
+        def hidden_matmuls(b, row_tiles):
+            for t in row_tiles:
+                hidden = slice(t * P, (t + 1) * P)
+                f_acc[b, t] = psum_f.tile([P, TOK], F32, name="f_acc")
+                for first, count in TOKEN_SLICES:
+                    cols = slice(first, first + count)
+                    nc.tensor.matmul_mx(
+                        out=f_acc[b, t][:, cols],
+                        lhsT=w1_codes[:, hidden].bitcast(FP8X4),
+                        lhsT_scale=w1_scales[:, hidden],
+                        rhs=h_codes[b][:, cols].bitcast(FP8X4),
+                        rhs_scale=h_scales[b][:, cols],
+                        start=True,
+                        stop=True,
+                    )
+
+        def hidden_relu(b, row_tiles):
+            if b not in f_planes:
+                f_planes[b] = work.tile([P, PACK, TOK], BF16, name="f_planes")
+            for t in row_tiles:
+                nc.scalar.activation(
+                    out=f_planes[b][:, t, :], in_=f_acc[b, t][:], func=ACT.Relu, bias=bias[:, t : t + 1], scale=1.0
+                )
+
+        def regroup_f(b):
+            f_grouped[b] = work.tile([P, TOK, PACK], BF16, align_bytes=64, name="f_grouped")
+            nc.vector.tensor_copy(
+                out=f_grouped[b][:].rearrange("p (c i) t -> p c t i", i=4),
+                in_=f_planes[b][:].rearrange("p t (c i) -> p c t i", i=4),
+            )
+
+        def quantise_f(b):
+            f_codes[b] = work.tile([P, TOK], U32, align_bytes=64, name="f_codes")
+            f_scales[b] = work.tile([P, TOK], U8, align_bytes=64, name="f_scales")
+            for first, count in TOKEN_SLICES:
+                quantise(f_grouped[b], f_codes[b], f_scales[b], first, count)
+
+        def differences(b):
+            for plus, minus in ((1, 0), (0, 2), (1, 2)):
+                z_diff[b, plus, minus] = psum_d.tile([P, H], F32, name="z_diff")
+                for token, codes, scales in ((plus, w_codes, w_scales), (minus, neg_w_codes, neg_w_scales)):
+                    tokens = slice(token * P, (token + 1) * P)
+                    nc.tensor.matmul_mx(
+                        out=z_diff[b, plus, minus][:],
+                        lhsT=f_codes[b][:, tokens].bitcast(FP8X4),
+                        lhsT_scale=f_scales[b][:, tokens],
+                        rhs=codes[:].bitcast(FP8X4),
+                        rhs_scale=scales[:],
+                        start=(token == plus),
+                        stop=(token == minus),
+                    )
+            h1_minus_h0[b] = psum_g.tile([P, H], F32, name="h1_minus_h0")
+            nc.tensor.matmul(out=h1_minus_h0[b][:], lhsT=ident_bf16[:], rhs=h_all[:, b, 1, :], start=True, stop=False)
+            nc.tensor.matmul(out=h1_minus_h0[b][:], lhsT=neg_ident_bf16[:], rhs=h_all[:, b, 0, :], start=False, stop=True)
+
+        def tanh_and_exps(b):
+            t01[b] = work.tile([P, H], F32, name="t01")
+            nc.scalar.activation(out=t01[b][:], in_=z_diff[b, 1, 0][:], func=ACT.Tanh, scale=0.5)
+            e_to_2[b] = work.tile([P, 2, H], F32, name="e_to_2")
+            for token in range(2):
+                nc.scalar.activation(out=e_to_2[b][:, token, :], in_=z_diff[b, token, 2][:], func=ACT.Exp)
+
+        def pair_and_sum(b):
+            nc.vector.tensor_tensor(out=share2[:, b, :], in0=e_to_2[b][:, 0, :], in1=e_to_2[b][:, 1, :], op=ALU.add)
+            nc.vector.scalar_tensor_tensor(
+                out=pair[:, b, :], in0=t01[b][:], scalar=1.0, in1=h1_minus_h0[b][:], op0=ALU.add, op1=ALU.mult
+            )
+            nc.vector.tensor_scalar_min(out=share2[:, b, :], in0=share2[:, b, :], scalar1=LN_CEILING)
+            nc.vector.scalar_tensor_tensor(
+                out=pair[:, b, :], in0=pair[:, b, :], scalar=0.5, in1=h_all[:, b, 0, :], op0=ALU.mult, op1=ALU.add
+            )
+            nc.vector.tensor_tensor(out=rest[:, b, :], in0=h_all[:, b, 2, :], in1=pair[:, b, :], op=ALU.subtract)
+
+        def log_of_sums(first, end):
+            nc.scalar.activation(out=share2[:, first:end, :], in_=share2[:, first:end, :], func=ACT.Ln, bias=1.0, scale=1.0)
+
+        def share_of_token_2(b):
+            nc.scalar.activation(out=share2[:, b, :], in_=share2[:, b, :], func=ACT.Exp, scale=-1.0)
+
+        def finish(first, end):
+            for b in range(first, end):
+                nc.vector.tensor_tensor(out=rest[:, b, :], in0=rest[:, b, :], in1=share2[:, b, :], op=ALU.mult)
+            for b in range(first, end):
+                nc.vector.tensor_tensor(out=rest[:, b, :], in0=rest[:, b, :], in1=pair[:, b, :], op=ALU.add)
+                nc.sync.dma_start(out=out[b], in_=rest[:, b, :])
+
+        def live(b):
+            return 0 <= b < BATCHES
+
+        w1_grouped, w1_codes, w1_scales = group_weight(w1_rows, "w1")
+        quantise(w1_grouped, w1_codes, w1_scales, 0, H)
+
+        bias_grouped = setup.tile([P, P, PACK], BF16)
+        dst, src = group_views(transpose_rows([bias_rows[:]]), 1, bias_grouped[:])
+        nc.scalar.copy(out=dst, in_=src)
+        bias = keep.tile([P, PACK], F32)
+        nc.vector.tensor_copy(out=bias[:], in_=bias_grouped[:, 0, :])
+
+        transpose_h(0)
+        group_h_tokens_01(0)
+        group_h_token_2(0)
+        w_grouped, w_codes, w_scales = group_weight(w_rows, "w")
+        quantise_h(0)
+        quantise(w_grouped, w_codes, w_scales, 0, H)
+        neg_w_grouped = setup.tile([P, H, PACK], BF16, align_bytes=64)
+        nc.vector.tensor_scalar_mul(out=neg_w_grouped[:], in0=w_grouped[:], scalar1=-1.0)
+        neg_w_codes = keep.tile([P, H], U32, align_bytes=64)
+        neg_w_scales = keep.tile([P, H], U8, align_bytes=64)
+        quantise(neg_w_grouped, neg_w_codes, neg_w_scales, 0, H)
+        transpose_h(1)
+        hidden_matmuls(0, FIRST_HALF)
+
+        logs_done = 0
+        shares_done = 0
+        finished = 0
+        for i in range(BATCHES + 2):
+            if live(i + 1):
+                group_h_token_2(i + 1)
+            if live(i - 2):
+                pair_and_sum(i - 2)
+            if live(i):
+                hidden_relu(i, FIRST_HALF)
+                hidden_matmuls(i, SECOND_HALF)
+            if live(i + 1):
+                group_h_tokens_01(i + 1)
+            if live(i):
+                hidden_relu(i, SECOND_HALF)
+            if live(i - 1):
+                differences(i - 1)
+                tanh_and_exps(i - 1)
+            if live(i + 1):
+                quantise_h(i + 1)
+            if live(i):
+                regroup_f(i)
+            if live(i + 2):
+                transpose_h(i + 2)
+            if live(i + 1):
+                hidden_matmuls(i + 1, FIRST_HALF)
+            group_is_full = live(i - 2) and ((i - 1) % LN_GROUP == 0 or i - 2 == BATCHES - 1)
+            if group_is_full:
+                for b in range(shares_done, logs_done):
+                    share_of_token_2(b)
+                shares_done = logs_done
+                log_of_sums(logs_done, i - 1)
+                logs_done = i - 1
+            elif shares_done < logs_done:
+                share_of_token_2(shares_done)
+                shares_done += 1
+            if live(i):
+                quantise_f(i)
+            if group_is_full:
+                finish(finished, shares_done)
+                finished = shares_done
+        for b in range(shares_done, BATCHES):
+            share_of_token_2(b)
+        finish(finished, BATCHES)

@@ -24,8 +24,7 @@ TOKEN_SLICES = ((0, 256), (256, 128))
 LN_GROUP = 7
 LN_CEILING = 2.0**60
 
-FIRST_HALF = (0, 1)
-SECOND_HALF = (2, 3)
+RING_BANKS = 7
 
 FLOPS = 2 * 2 * BATCHES * TOK * H * H
 
@@ -36,9 +35,7 @@ def tile_blocksa_pa_t_kernel(tc, h, s2t_W1_w, s2t_W1_b, s2t_W_w, out):
         keep = ctx.enter_context(tc.tile_pool(name="keep", bufs=1))
         setup = ctx.enter_context(tc.tile_pool(name="setup", bufs=1))
         work = ctx.enter_context(tc.tile_pool(name="work", bufs=2))
-        psum_t = ctx.enter_context(tc.psum_pool(name="psum_t", bufs=2))
-        psum_f = ctx.enter_context(tc.psum_pool(name="psum_f", bufs=2))
-        psum_d = ctx.enter_context(tc.psum_pool(name="psum_d", bufs=3))
+        ring = ctx.enter_context(tc.psum_pool(name="ring", bufs=RING_BANKS))
         psum_g = ctx.enter_context(tc.psum_pool(name="psum_g", bufs=1))
         ctx.enter_context(tc.manual_schedule())
 
@@ -65,7 +62,7 @@ def tile_blocksa_pa_t_kernel(tc, h, s2t_W1_w, s2t_W1_b, s2t_W_w, out):
         nc.vector.tensor_scalar_mul(out=neg_ident_bf16[:], in0=ident_f32[:], scalar1=-1.0)
 
         def transpose_rows(row_tiles):
-            bank = psum_t.tile([P, 2, HALVES, P], F32)
+            bank = ring.tile([P, 2, HALVES, P], F32, name="bank")
             for a, rows in enumerate(row_tiles):
                 words = rows.bitcast(F32)
                 for u in range(HALVES):
@@ -122,10 +119,10 @@ def tile_blocksa_pa_t_kernel(tc, h, s2t_W1_w, s2t_W1_b, s2t_W_w, out):
             for first, count in TOKEN_SLICES:
                 quantise(h_grouped[b], h_codes[b], h_scales[b], first, count)
 
-        def hidden_matmuls(b, row_tiles):
-            for t in row_tiles:
+        def hidden_matmuls(b):
+            for t in range(PACK):
                 hidden = slice(t * P, (t + 1) * P)
-                f_acc[b, t] = psum_f.tile([P, TOK], F32, name="f_acc")
+                f_acc[b, t] = ring.tile([P, TOK], F32, name="bank")
                 for first, count in TOKEN_SLICES:
                     cols = slice(first, first + count)
                     nc.tensor.matmul_mx(
@@ -138,10 +135,9 @@ def tile_blocksa_pa_t_kernel(tc, h, s2t_W1_w, s2t_W1_b, s2t_W_w, out):
                         stop=True,
                     )
 
-        def hidden_relu(b, row_tiles):
-            if b not in f_planes:
-                f_planes[b] = work.tile([P, PACK, TOK], BF16, name="f_planes")
-            for t in row_tiles:
+        def hidden_relu(b):
+            f_planes[b] = work.tile([P, PACK, TOK], BF16, name="f_planes")
+            for t in range(PACK):
                 nc.scalar.activation(
                     out=f_planes[b][:, t, :], in_=f_acc[b, t][:], func=ACT.Relu, bias=bias[:, t : t + 1], scale=1.0
                 )
@@ -161,7 +157,7 @@ def tile_blocksa_pa_t_kernel(tc, h, s2t_W1_w, s2t_W1_b, s2t_W_w, out):
 
         def differences(b):
             for plus, minus in ((1, 0), (0, 2), (1, 2)):
-                z_diff[b, plus, minus] = psum_d.tile([P, H], F32, name="z_diff")
+                z_diff[b, plus, minus] = ring.tile([P, H], F32, name="bank")
                 for token, codes, scales in ((plus, w_codes, w_scales), (minus, neg_w_codes, neg_w_scales)):
                     tokens = slice(token * P, (token + 1) * P)
                     nc.tensor.matmul_mx(
@@ -184,16 +180,25 @@ def tile_blocksa_pa_t_kernel(tc, h, s2t_W1_w, s2t_W1_b, s2t_W_w, out):
             for token in range(2):
                 nc.scalar.activation(out=e_to_2[b][:, token, :], in_=z_diff[b, token, 2][:], func=ACT.Exp)
 
-        def pair_and_sum(b):
+        def sum_and_product(b):
             nc.vector.tensor_tensor(out=share2[:, b, :], in0=e_to_2[b][:, 0, :], in1=e_to_2[b][:, 1, :], op=ALU.add)
             nc.vector.scalar_tensor_tensor(
                 out=pair[:, b, :], in0=t01[b][:], scalar=1.0, in1=h1_minus_h0[b][:], op0=ALU.add, op1=ALU.mult
             )
             nc.vector.tensor_scalar_min(out=share2[:, b, :], in0=share2[:, b, :], scalar1=LN_CEILING)
+
+        def pair_and_rest(first, end):
             nc.vector.scalar_tensor_tensor(
-                out=pair[:, b, :], in0=pair[:, b, :], scalar=0.5, in1=h_all[:, b, 0, :], op0=ALU.mult, op1=ALU.add
+                out=pair[:, first:end, :],
+                in0=pair[:, first:end, :],
+                scalar=0.5,
+                in1=h_all[:, first:end, 0, :],
+                op0=ALU.mult,
+                op1=ALU.add,
             )
-            nc.vector.tensor_tensor(out=rest[:, b, :], in0=h_all[:, b, 2, :], in1=pair[:, b, :], op=ALU.subtract)
+            nc.vector.tensor_tensor(
+                out=rest[:, first:end, :], in0=h_all[:, first:end, 2, :], in1=pair[:, first:end, :], op=ALU.subtract
+            )
 
         def log_of_sums(first, end):
             nc.scalar.activation(out=share2[:, first:end, :], in_=share2[:, first:end, :], func=ACT.Ln, bias=1.0, scale=1.0)
@@ -201,12 +206,18 @@ def tile_blocksa_pa_t_kernel(tc, h, s2t_W1_w, s2t_W1_b, s2t_W_w, out):
         def share_of_token_2(b):
             nc.scalar.activation(out=share2[:, b, :], in_=share2[:, b, :], func=ACT.Exp, scale=-1.0)
 
+        def weigh_rest(b):
+            nc.vector.tensor_tensor(out=rest[:, b, :], in0=rest[:, b, :], in1=share2[:, b, :], op=ALU.mult)
+
+        def add_pair_and_store(b):
+            nc.vector.tensor_tensor(out=rest[:, b, :], in0=rest[:, b, :], in1=pair[:, b, :], op=ALU.add)
+            nc.sync.dma_start(out=out[b], in_=rest[:, b, :])
+
         def finish(first, end):
             for b in range(first, end):
-                nc.vector.tensor_tensor(out=rest[:, b, :], in0=rest[:, b, :], in1=share2[:, b, :], op=ALU.mult)
+                weigh_rest(b)
             for b in range(first, end):
-                nc.vector.tensor_tensor(out=rest[:, b, :], in0=rest[:, b, :], in1=pair[:, b, :], op=ALU.add)
-                nc.sync.dma_start(out=out[b], in_=rest[:, b, :])
+                add_pair_and_store(b)
 
         def live(b):
             return 0 <= b < BATCHES
@@ -232,49 +243,52 @@ def tile_blocksa_pa_t_kernel(tc, h, s2t_W1_w, s2t_W1_b, s2t_W_w, out):
         neg_w_scales = keep.tile([P, H], U8, align_bytes=64)
         quantise(neg_w_grouped, neg_w_codes, neg_w_scales, 0, H)
         transpose_h(1)
-        hidden_matmuls(0, FIRST_HALF)
+        hidden_matmuls(0)
 
         logs_done = 0
         shares_done = 0
         finished = 0
         for i in range(BATCHES + 2):
             if live(i + 1):
+                group_h_tokens_01(i + 1)
                 group_h_token_2(i + 1)
             if live(i - 2):
-                pair_and_sum(i - 2)
-            if live(i):
-                hidden_relu(i, FIRST_HALF)
-                hidden_matmuls(i, SECOND_HALF)
-            if live(i + 1):
-                group_h_tokens_01(i + 1)
-            if live(i):
-                hidden_relu(i, SECOND_HALF)
+                sum_and_product(i - 2)
             if live(i - 1):
                 differences(i - 1)
-                tanh_and_exps(i - 1)
             if live(i + 1):
                 quantise_h(i + 1)
             if live(i):
-                regroup_f(i)
+                hidden_relu(i)
             if live(i + 2):
                 transpose_h(i + 2)
+            if live(i):
+                regroup_f(i)
+            if live(i - 1):
+                tanh_and_exps(i - 1)
             if live(i + 1):
-                hidden_matmuls(i + 1, FIRST_HALF)
+                hidden_matmuls(i + 1)
+            one_to_finish = finished < shares_done
+            if one_to_finish:
+                weigh_rest(finished)
+            if live(i):
+                quantise_f(i)
+            if one_to_finish:
+                add_pair_and_store(finished)
+                finished += 1
             group_is_full = live(i - 2) and ((i - 1) % LN_GROUP == 0 or i - 2 == BATCHES - 1)
             if group_is_full:
                 for b in range(shares_done, logs_done):
                     share_of_token_2(b)
                 shares_done = logs_done
                 log_of_sums(logs_done, i - 1)
+                pair_and_rest(logs_done, i - 1)
                 logs_done = i - 1
+                finish(finished, shares_done)
+                finished = shares_done
             elif shares_done < logs_done:
                 share_of_token_2(shares_done)
                 shares_done += 1
-            if live(i):
-                quantise_f(i)
-            if group_is_full:
-                finish(finished, shares_done)
-                finished = shares_done
         for b in range(shares_done, BATCHES):
             share_of_token_2(b)
         finish(finished, BATCHES)

@@ -37,7 +37,6 @@ def tile_blocksa_pa_t_kernel(tc, h, s2t_W1_w, s2t_W1_b, s2t_W_w, out):
         work = ctx.enter_context(tc.tile_pool(name="work", bufs=2))
         ring = ctx.enter_context(tc.psum_pool(name="ring", bufs=RING_BANKS))
         psum_g = ctx.enter_context(tc.psum_pool(name="psum_g", bufs=1))
-        ctx.enter_context(tc.manual_schedule())
 
         w1_rows = setup.tile([P, PACK, H], BF16)
         nc.sync.dma_start(

@@ -21,8 +21,6 @@ TOK = TOKENS * P
 
 TOKEN_SLICES = ((0, 256), (256, 128))
 
-LN_GROUP = 7
-LN_CEILING = 2.0**60
 
 RING_BANKS = 7
 
@@ -32,6 +30,7 @@ FLOPS = 2 * 2 * BATCHES * TOK * H * H
 def tile_blocksa_pa_t_kernel(tc, h, s2t_W1_w, s2t_W1_b, s2t_W_w, out):
     nc = tc.nc
     with ExitStack() as ctx:
+        ctx.enter_context(tc.manual_schedule(engines={mybir.EngineType.Activation}))
         keep = ctx.enter_context(tc.tile_pool(name="keep", bufs=1))
         setup = ctx.enter_context(tc.tile_pool(name="setup", bufs=1))
         work = ctx.enter_context(tc.tile_pool(name="work", bufs=2))
@@ -184,26 +183,22 @@ def tile_blocksa_pa_t_kernel(tc, h, s2t_W1_w, s2t_W1_b, s2t_W_w, out):
             nc.vector.scalar_tensor_tensor(
                 out=pair[:, b, :], in0=t01[b][:], scalar=1.0, in1=h1_minus_h0[b][:], op0=ALU.add, op1=ALU.mult
             )
-            nc.vector.tensor_scalar_min(out=share2[:, b, :], in0=share2[:, b, :], scalar1=LN_CEILING)
 
-        def pair_and_rest(first, end):
+        def pair_of_01(b):
             nc.vector.scalar_tensor_tensor(
-                out=pair[:, first:end, :],
-                in0=pair[:, first:end, :],
-                scalar=0.5,
-                in1=h_all[:, first:end, 0, :],
-                op0=ALU.mult,
-                op1=ALU.add,
-            )
-            nc.vector.tensor_tensor(
-                out=rest[:, first:end, :], in0=h_all[:, first:end, 2, :], in1=pair[:, first:end, :], op=ALU.subtract
+                out=pair[:, b, :], in0=pair[:, b, :], scalar=0.5, in1=h_all[:, b, 0, :], op0=ALU.mult, op1=ALU.add
             )
 
-        def log_of_sums(first, end):
-            nc.scalar.activation(out=share2[:, first:end, :], in_=share2[:, first:end, :], func=ACT.Ln, bias=1.0, scale=1.0)
+        def rest_of_2(b):
+            nc.vector.tensor_tensor(out=rest[:, b, :], in0=h_all[:, b, 2, :], in1=pair[:, b, :], op=ALU.subtract)
+
+        def root_of_share_2(b):
+            nc.scalar.activation(
+                out=share2[:, b, :], in_=share2[:, b, :], func=ACT.Abs_reciprocal_sqrt, bias=1.0, scale=1.0
+            )
 
         def share_of_token_2(b):
-            nc.scalar.activation(out=share2[:, b, :], in_=share2[:, b, :], func=ACT.Exp, scale=-1.0)
+            nc.scalar.activation(out=share2[:, b, :], in_=share2[:, b, :], func=ACT.Square)
 
         def weigh_rest(b):
             nc.vector.tensor_tensor(out=rest[:, b, :], in0=rest[:, b, :], in1=share2[:, b, :], op=ALU.mult)
@@ -211,12 +206,6 @@ def tile_blocksa_pa_t_kernel(tc, h, s2t_W1_w, s2t_W1_b, s2t_W_w, out):
         def add_pair_and_store(b):
             nc.vector.tensor_tensor(out=rest[:, b, :], in0=rest[:, b, :], in1=pair[:, b, :], op=ALU.add)
             nc.sync.dma_start(out=out[b], in_=rest[:, b, :])
-
-        def finish(first, end):
-            for b in range(first, end):
-                weigh_rest(b)
-            for b in range(first, end):
-                add_pair_and_store(b)
 
         def live(b):
             return 0 <= b < BATCHES
@@ -244,9 +233,6 @@ def tile_blocksa_pa_t_kernel(tc, h, s2t_W1_w, s2t_W1_b, s2t_W_w, out):
         transpose_h(1)
         hidden_matmuls(0)
 
-        logs_done = 0
-        shares_done = 0
-        finished = 0
         for i in range(BATCHES + 2):
             if live(i + 1):
                 group_h_tokens_01(i + 1)
@@ -267,27 +253,18 @@ def tile_blocksa_pa_t_kernel(tc, h, s2t_W1_w, s2t_W1_b, s2t_W_w, out):
                 tanh_and_exps(i - 1)
             if live(i + 1):
                 hidden_matmuls(i + 1)
-            one_to_finish = finished < shares_done
-            if one_to_finish:
-                weigh_rest(finished)
+            if live(i - 2):
+                pair_of_01(i - 2)
             if live(i):
                 quantise_f(i)
-            if one_to_finish:
-                add_pair_and_store(finished)
-                finished += 1
-            group_is_full = live(i - 2) and ((i - 1) % LN_GROUP == 0 or i - 2 == BATCHES - 1)
-            if group_is_full:
-                for b in range(shares_done, logs_done):
-                    share_of_token_2(b)
-                shares_done = logs_done
-                log_of_sums(logs_done, i - 1)
-                pair_and_rest(logs_done, i - 1)
-                logs_done = i - 1
-                finish(finished, shares_done)
-                finished = shares_done
-            elif shares_done < logs_done:
-                share_of_token_2(shares_done)
-                shares_done += 1
-        for b in range(shares_done, BATCHES):
-            share_of_token_2(b)
-        finish(finished, BATCHES)
+            if live(i - 2):
+                rest_of_2(i - 2)
+
+        for i in range(BATCHES + 2):
+            if live(i):
+                root_of_share_2(i)
+            if live(i - 1):
+                share_of_token_2(i - 1)
+                weigh_rest(i - 1)
+            if live(i - 2):
+                add_pair_and_store(i - 2)

@@ -24,6 +24,10 @@ TOKEN_SLICES = ((0, 256), (256, 128))
 
 RING_BANKS = 7
 
+PE_BATCHES = (4, 8, 12)
+
+LAG = 4
+
 FLOPS = 2 * 2 * BATCHES * TOK * H * H
 
 
@@ -37,18 +41,21 @@ def tile_blocksa_pa_t_kernel(tc, h, s2t_W1_w, s2t_W1_b, s2t_W_w, out):
         ring = ctx.enter_context(tc.psum_pool(name="ring", bufs=RING_BANKS))
         psum_g = ctx.enter_context(tc.psum_pool(name="psum_g", bufs=1))
 
-        w1_rows = setup.tile([P, PACK, H], BF16)
-        nc.sync.dma_start(
-            out=w1_rows[:].rearrange("p (u e) k -> p u (e k)", u=HALVES),
-            in_=s2t_W1_w.rearrange("(u p e) k -> p u (e k)", u=HALVES, e=2),
-        )
+        w1_rows = []
+        for u in range(HALVES):
+            half = setup.tile([P, 2, H], BF16, name="w1_rows_%d" % u)
+            nc.sync.dma_start(out=half[:], in_=s2t_W1_w[2 * u * P : 2 * (u + 1) * P].rearrange("(p e) k -> p e k", e=2))
+            w1_rows.append(half)
+        h_all = keep.tile([P, BATCHES, TOKENS, H], BF16)
+        nc.sync.dma_start(out=h_all[:, 0], in_=h[0])
         bias_rows = setup.tile([P, H], BF16)
         nc.vector.memset(bias_rows[:], 0.0)
         nc.sync.dma_start(out=bias_rows[0:1, :], in_=s2t_W1_b.rearrange("(o k) -> o k", o=1))
-        h_all = keep.tile([P, BATCHES, TOKENS, H], BF16)
-        nc.sync.dma_start(out=h_all[:, 0], in_=h[0])
-        w_rows = setup.tile([P, PACK, H], BF16)
-        nc.sync.dma_start(out=w_rows[:], in_=s2t_W_w.rearrange("(a p) k -> p a k", p=P))
+        w_rows = []
+        for a in range(HALVES):
+            half = setup.tile([P, 2, H], BF16, name="w_rows_%d" % a)
+            nc.sync.dma_start(out=half[:], in_=s2t_W_w[2 * a * P : 2 * (a + 1) * P].rearrange("(i p) k -> p i k", p=P))
+            w_rows.append(half)
         for b in range(1, BATCHES):
             nc.sync.dma_start(out=h_all[:, b], in_=h[b])
 
@@ -58,6 +65,10 @@ def tile_blocksa_pa_t_kernel(tc, h, s2t_W1_w, s2t_W1_b, s2t_W_w, out):
         nc.vector.tensor_copy(out=ident_bf16[:], in_=ident_f32[:])
         neg_ident_bf16 = keep.tile([P, P], BF16)
         nc.vector.tensor_scalar_mul(out=neg_ident_bf16[:], in0=ident_f32[:], scalar1=-1.0)
+        half_bf16 = keep.tile([P, P], BF16)
+        nc.vector.tensor_scalar_mul(out=half_bf16[:], in0=ident_f32[:], scalar1=0.5)
+        neg_half_bf16 = keep.tile([P, P], BF16)
+        nc.vector.tensor_scalar_mul(out=neg_half_bf16[:], in0=ident_f32[:], scalar1=-0.5)
 
         def transpose_rows(row_tiles):
             bank = ring.tile([P, 2, HALVES, P], F32, name="bank")
@@ -84,20 +95,22 @@ def tile_blocksa_pa_t_kernel(tc, h, s2t_W1_w, s2t_W1_b, s2t_W_w, out):
 
         def group_weight(rows, name):
             grouped = setup.tile([P, H, PACK], BF16, align_bytes=64, name=name + "_grouped")
-            for a in range(0, PACK, 2):
-                bank = transpose_rows([rows[:, a, :], rows[:, a + 1, :]])
-                dst, src = group_views(bank, 2, grouped[:, a * P : (a + 2) * P, :])
-                nc.scalar.copy(out=dst, in_=src)
+            for a, half in enumerate(rows):
+                bank = transpose_rows([half[:, 0, :], half[:, 1, :]])
+                dst, src = group_views(bank, 2, grouped[:, 2 * a * P : 2 * (a + 1) * P, :])
+                if a == 0:
+                    nc.scalar.copy(out=dst, in_=src)
+                else:
+                    nc.vector.tensor_copy(out=dst, in_=src)
             codes = keep.tile([P, H], U32, align_bytes=64, name=name + "_codes")
             scales = keep.tile([P, H], U8, align_bytes=64, name=name + "_scales")
             return grouped, codes, scales
 
         h_banks, h_grouped, h_codes, h_scales = {}, {}, {}, {}
         f_acc, f_planes, f_grouped, f_codes, f_scales = {}, {}, {}, {}, {}
-        z_diff, h1_minus_h0, t01, e_to_2 = {}, {}, {}, {}
+        z_diff, h1_minus_h0, h0_minus_h2, t01, e_to_2 = {}, {}, {}, {}, {}
         share2 = keep.tile([P, BATCHES, H], F32)
-        pair = keep.tile([P, BATCHES, H], F32)
-        rest = keep.tile([P, BATCHES, H], F32)
+        excess = keep.tile([P, BATCHES, H], F32)
 
         def transpose_h(b):
             h_banks[b] = (transpose_rows([h_all[:, b, 0, :], h_all[:, b, 1, :]]), transpose_rows([h_all[:, b, 2, :]]))
@@ -109,7 +122,10 @@ def tile_blocksa_pa_t_kernel(tc, h, s2t_W1_w, s2t_W1_b, s2t_W_w, out):
 
         def group_h_token_2(b):
             dst, src = group_views(h_banks[b][1], 1, h_grouped[b][:, 2 * P : 3 * P, :])
-            nc.vector.tensor_copy(out=dst, in_=src)
+            if b % 2 == 0:
+                nc.vector.tensor_copy(out=dst, in_=src)
+            else:
+                nc.scalar.copy(out=dst, in_=src)
 
         def quantise_h(b):
             h_codes[b] = work.tile([P, TOK], U32, align_bytes=64, name="h_codes")
@@ -168,8 +184,8 @@ def tile_blocksa_pa_t_kernel(tc, h, s2t_W1_w, s2t_W1_b, s2t_W_w, out):
                         stop=(token == minus),
                     )
             h1_minus_h0[b] = psum_g.tile([P, H], F32, name="h1_minus_h0")
-            nc.tensor.matmul(out=h1_minus_h0[b][:], lhsT=ident_bf16[:], rhs=h_all[:, b, 1, :], start=True, stop=False)
-            nc.tensor.matmul(out=h1_minus_h0[b][:], lhsT=neg_ident_bf16[:], rhs=h_all[:, b, 0, :], start=False, stop=True)
+            nc.tensor.matmul(out=h1_minus_h0[b][:], lhsT=half_bf16[:], rhs=h_all[:, b, 1, :], start=True, stop=False)
+            nc.tensor.matmul(out=h1_minus_h0[b][:], lhsT=neg_half_bf16[:], rhs=h_all[:, b, 0, :], start=False, stop=True)
 
         def tanh_and_exps(b):
             t01[b] = work.tile([P, H], F32, name="t01")
@@ -181,16 +197,24 @@ def tile_blocksa_pa_t_kernel(tc, h, s2t_W1_w, s2t_W1_b, s2t_W_w, out):
         def sum_and_product(b):
             nc.vector.tensor_tensor(out=share2[:, b, :], in0=e_to_2[b][:, 0, :], in1=e_to_2[b][:, 1, :], op=ALU.add)
             nc.vector.scalar_tensor_tensor(
-                out=pair[:, b, :], in0=t01[b][:], scalar=1.0, in1=h1_minus_h0[b][:], op0=ALU.add, op1=ALU.mult
+                out=excess[:, b, :], in0=t01[b][:], scalar=1.0, in1=h1_minus_h0[b][:], op0=ALU.add, op1=ALU.mult
             )
 
-        def pair_of_01(b):
-            nc.vector.scalar_tensor_tensor(
-                out=pair[:, b, :], in0=pair[:, b, :], scalar=0.5, in1=h_all[:, b, 0, :], op0=ALU.mult, op1=ALU.add
-            )
+        def token_0_minus_2(b):
+            h0_minus_h2[b] = psum_g.tile([P, H], F32, name="h1_minus_h0")
+            nc.tensor.matmul(out=h0_minus_h2[b][:], lhsT=ident_bf16[:], rhs=h_all[:, b, 0, :], start=True, stop=False)
+            nc.tensor.matmul(out=h0_minus_h2[b][:], lhsT=neg_ident_bf16[:], rhs=h_all[:, b, 2, :], start=False, stop=True)
 
-        def rest_of_2(b):
-            nc.vector.tensor_tensor(out=rest[:, b, :], in0=h_all[:, b, 2, :], in1=pair[:, b, :], op=ALU.subtract)
+        def add_token_0(b):
+            if b in PE_BATCHES:
+                token_0_minus_2(b)
+                nc.vector.tensor_tensor(out=excess[:, b, :], in0=excess[:, b, :], in1=h0_minus_h2[b][:], op=ALU.add)
+            else:
+                nc.vector.tensor_tensor(out=excess[:, b, :], in0=excess[:, b, :], in1=h_all[:, b, 0, :], op=ALU.add)
+
+        def subtract_token_2(b):
+            if b not in PE_BATCHES:
+                nc.vector.tensor_tensor(out=excess[:, b, :], in0=excess[:, b, :], in1=h_all[:, b, 2, :], op=ALU.subtract)
 
         def root_of_share_2(b):
             nc.scalar.activation(
@@ -200,38 +224,40 @@ def tile_blocksa_pa_t_kernel(tc, h, s2t_W1_w, s2t_W1_b, s2t_W_w, out):
         def share_of_token_2(b):
             nc.scalar.activation(out=share2[:, b, :], in_=share2[:, b, :], func=ACT.Square)
 
-        def weigh_rest(b):
-            nc.vector.tensor_tensor(out=rest[:, b, :], in0=rest[:, b, :], in1=share2[:, b, :], op=ALU.mult)
+        def weigh_excess(b):
+            nc.vector.scalar_tensor_tensor(
+                out=excess[:, b, :], in0=share2[:, b, :], scalar=-1.0, in1=excess[:, b, :], op0=ALU.add, op1=ALU.mult
+            )
 
-        def add_pair_and_store(b):
-            nc.vector.tensor_tensor(out=rest[:, b, :], in0=rest[:, b, :], in1=pair[:, b, :], op=ALU.add)
-            nc.sync.dma_start(out=out[b], in_=rest[:, b, :])
+        def subtract_and_store(b):
+            nc.vector.tensor_tensor(out=excess[:, b, :], in0=h_all[:, b, 2, :], in1=excess[:, b, :], op=ALU.subtract)
+            nc.sync.dma_start(out=out[b], in_=excess[:, b, :])
 
         def live(b):
             return 0 <= b < BATCHES
 
         w1_grouped, w1_codes, w1_scales = group_weight(w1_rows, "w1")
-        quantise(w1_grouped, w1_codes, w1_scales, 0, H)
-
-        bias_grouped = setup.tile([P, P, PACK], BF16)
-        dst, src = group_views(transpose_rows([bias_rows[:]]), 1, bias_grouped[:])
-        nc.scalar.copy(out=dst, in_=src)
-        bias = keep.tile([P, PACK], F32)
-        nc.vector.tensor_copy(out=bias[:], in_=bias_grouped[:, 0, :])
-
         transpose_h(0)
         group_h_tokens_01(0)
+        quantise(w1_grouped, w1_codes, w1_scales, 0, H)
         group_h_token_2(0)
-        w_grouped, w_codes, w_scales = group_weight(w_rows, "w")
+
+        bias_words = transpose_rows([bias_rows[:]])
+        bias_grouped = setup.tile([P, PACK], BF16)
+        nc.scalar.copy(out=bias_grouped[:].bitcast(F32), in_=bias_words[:, 0, :, 0])
+        bias = keep.tile([P, PACK], F32)
+        nc.vector.tensor_copy(out=bias[:], in_=bias_grouped[:])
+
         quantise_h(0)
+        w_grouped, w_codes, w_scales = group_weight(w_rows, "w")
+        transpose_h(1)
+        hidden_matmuls(0)
         quantise(w_grouped, w_codes, w_scales, 0, H)
         neg_w_grouped = setup.tile([P, H, PACK], BF16, align_bytes=64)
         nc.vector.tensor_scalar_mul(out=neg_w_grouped[:], in0=w_grouped[:], scalar1=-1.0)
         neg_w_codes = keep.tile([P, H], U32, align_bytes=64)
         neg_w_scales = keep.tile([P, H], U8, align_bytes=64)
         quantise(neg_w_grouped, neg_w_codes, neg_w_scales, 0, H)
-        transpose_h(1)
-        hidden_matmuls(0)
 
         for i in range(BATCHES + 2):
             if live(i + 1):
@@ -254,17 +280,19 @@ def tile_blocksa_pa_t_kernel(tc, h, s2t_W1_w, s2t_W1_b, s2t_W_w, out):
             if live(i + 1):
                 hidden_matmuls(i + 1)
             if live(i - 2):
-                pair_of_01(i - 2)
+                add_token_0(i - 2)
             if live(i):
                 quantise_f(i)
-            if live(i - 2):
-                rest_of_2(i - 2)
+            if live(i - 2 - LAG):
+                subtract_token_2(i - 2 - LAG)
+        for b in range(BATCHES - LAG, BATCHES):
+            subtract_token_2(b)
 
         for i in range(BATCHES + 2):
             if live(i):
                 root_of_share_2(i)
             if live(i - 1):
                 share_of_token_2(i - 1)
-                weigh_rest(i - 1)
+                weigh_excess(i - 1)
             if live(i - 2):
-                add_pair_and_store(i - 2)
+                subtract_and_store(i - 2)

@@ -95,6 +95,8 @@ def tile_blocksa_pa_t_kernel(tc, h, s2t_W1_w, s2t_W1_b, s2t_W_w, out):
 
         def group_weight(rows, name):
             grouped = setup.tile([P, H, PACK], BF16, align_bytes=64, name=name + "_grouped")
+            codes = keep.tile([P, H], U32, align_bytes=64, name=name + "_codes")
+            scales = keep.tile([P, H], U8, align_bytes=64, name=name + "_scales")
             for a, half in enumerate(rows):
                 bank = transpose_rows([half[:, 0, :], half[:, 1, :]])
                 dst, src = group_views(bank, 2, grouped[:, 2 * a * P : 2 * (a + 1) * P, :])
@@ -102,8 +104,6 @@ def tile_blocksa_pa_t_kernel(tc, h, s2t_W1_w, s2t_W1_b, s2t_W_w, out):
                     nc.scalar.copy(out=dst, in_=src)
                 else:
                     nc.vector.tensor_copy(out=dst, in_=src)
-            codes = keep.tile([P, H], U32, align_bytes=64, name=name + "_codes")
-            scales = keep.tile([P, H], U8, align_bytes=64, name=name + "_scales")
             return grouped, codes, scales
 
         h_banks, h_grouped, h_codes, h_scales = {}, {}, {}, {}
@@ -158,10 +158,12 @@ def tile_blocksa_pa_t_kernel(tc, h, s2t_W1_w, s2t_W1_b, s2t_W_w, out):
 
         def regroup_f(b):
             f_grouped[b] = work.tile([P, TOK, PACK], BF16, align_bytes=64, name="f_grouped")
-            nc.vector.tensor_copy(
-                out=f_grouped[b][:].rearrange("p (c i) t -> p c t i", i=4),
-                in_=f_planes[b][:].rearrange("p t (c i) -> p c t i", i=4),
-            )
+            for first, count in TOKEN_SLICES if b == BATCHES - 1 else ((0, TOK),):
+                cols = slice(first, first + count)
+                nc.vector.tensor_copy(
+                    out=f_grouped[b][:, cols, :].rearrange("p (c i) t -> p c t i", i=8),
+                    in_=f_planes[b][:, :, cols].rearrange("p t (c i) -> p c t i", i=8),
+                )
 
         def quantise_f(b):
             f_codes[b] = work.tile([P, TOK], U32, align_bytes=64, name="f_codes")
@@ -216,22 +218,27 @@ def tile_blocksa_pa_t_kernel(tc, h, s2t_W1_w, s2t_W1_b, s2t_W_w, out):
             if b not in PE_BATCHES:
                 nc.vector.tensor_tensor(out=excess[:, b, :], in0=excess[:, b, :], in1=h_all[:, b, 2, :], op=ALU.subtract)
 
-        def root_of_share_2(b):
+        def root_of_share_2(b, cols):
             nc.scalar.activation(
-                out=share2[:, b, :], in_=share2[:, b, :], func=ACT.Abs_reciprocal_sqrt, bias=1.0, scale=1.0
+                out=share2[:, b, cols], in_=share2[:, b, cols], func=ACT.Abs_reciprocal_sqrt, bias=1.0, scale=1.0
             )
 
-        def share_of_token_2(b):
-            nc.scalar.activation(out=share2[:, b, :], in_=share2[:, b, :], func=ACT.Square)
+        def share_of_token_2(b, cols):
+            nc.scalar.activation(out=share2[:, b, cols], in_=share2[:, b, cols], func=ACT.Square)
 
-        def weigh_excess(b):
+        def weigh_excess(b, cols):
             nc.vector.scalar_tensor_tensor(
-                out=excess[:, b, :], in0=share2[:, b, :], scalar=-1.0, in1=excess[:, b, :], op0=ALU.add, op1=ALU.mult
+                out=excess[:, b, cols],
+                in0=share2[:, b, cols],
+                scalar=-1.0,
+                in1=excess[:, b, cols],
+                op0=ALU.add,
+                op1=ALU.mult,
             )
 
-        def subtract_and_store(b):
-            nc.vector.tensor_tensor(out=excess[:, b, :], in0=h_all[:, b, 2, :], in1=excess[:, b, :], op=ALU.subtract)
-            nc.sync.dma_start(out=out[b], in_=excess[:, b, :])
+        def subtract_and_store(b, cols):
+            nc.vector.tensor_tensor(out=excess[:, b, cols], in0=h_all[:, b, 2, cols], in1=excess[:, b, cols], op=ALU.subtract)
+            nc.sync.dma_start(out=out[b, :, cols], in_=excess[:, b, cols])
 
         def live(b):
             return 0 <= b < BATCHES
@@ -239,7 +246,8 @@ def tile_blocksa_pa_t_kernel(tc, h, s2t_W1_w, s2t_W1_b, s2t_W_w, out):
         w1_grouped, w1_codes, w1_scales = group_weight(w1_rows, "w1")
         transpose_h(0)
         group_h_tokens_01(0)
-        quantise(w1_grouped, w1_codes, w1_scales, 0, H)
+        for a in range(HALVES):
+            quantise(w1_grouped, w1_codes, w1_scales, 2 * a * P, 2 * P)
         group_h_token_2(0)
 
         bias_words = transpose_rows([bias_rows[:]])
@@ -288,11 +296,16 @@ def tile_blocksa_pa_t_kernel(tc, h, s2t_W1_w, s2t_W1_b, s2t_W_w, out):
         for b in range(BATCHES - LAG, BATCHES):
             subtract_token_2(b)
 
-        for i in range(BATCHES + 2):
-            if live(i):
-                root_of_share_2(i)
-            if live(i - 1):
-                share_of_token_2(i - 1)
-                weigh_excess(i - 1)
-            if live(i - 2):
-                subtract_and_store(i - 2)
+        pieces = []
+        for b in range(BATCHES):
+            count = 2 if b in (0, BATCHES - 1) else 1
+            for part in range(count):
+                pieces.append((b, slice(part * H // count, (part + 1) * H // count)))
+        for i in range(len(pieces) + 2):
+            if i < len(pieces):
+                root_of_share_2(*pieces[i])
+            if 1 <= i <= len(pieces):
+                share_of_token_2(*pieces[i - 1])
+                weigh_excess(*pieces[i - 1])
+            if i >= 2:
+                subtract_and_store(*pieces[i - 2])

@@ -122,10 +122,7 @@ def tile_blocksa_pa_t_kernel(tc, h, s2t_W1_w, s2t_W1_b, s2t_W_w, out):
 
         def group_h_token_2(b):
             dst, src = group_views(h_banks[b][1], 1, h_grouped[b][:, 2 * P : 3 * P, :])
-            if b % 2 == 0:
-                nc.vector.tensor_copy(out=dst, in_=src)
-            else:
-                nc.scalar.copy(out=dst, in_=src)
+            nc.vector.tensor_copy(out=dst, in_=src)
 
         def quantise_h(b):
             h_codes[b] = work.tile([P, TOK], U32, align_bytes=64, name="h_codes")

@@ -22,11 +22,11 @@ TOK = TOKENS * P
 TOKEN_SLICES = ((0, 256), (256, 128))
 
 
-RING_BANKS = 7
+RING_BANKS = 6
 
 PE_BATCHES = (4, 8, 12)
 
-LAG = 4
+LAG = 6
 
 FLOPS = 2 * 2 * BATCHES * TOK * H * H
 
@@ -39,7 +39,7 @@ def tile_blocksa_pa_t_kernel(tc, h, s2t_W1_w, s2t_W1_b, s2t_W_w, out):
         setup = ctx.enter_context(tc.tile_pool(name="setup", bufs=1))
         work = ctx.enter_context(tc.tile_pool(name="work", bufs=2))
         ring = ctx.enter_context(tc.psum_pool(name="ring", bufs=RING_BANKS))
-        psum_g = ctx.enter_context(tc.psum_pool(name="psum_g", bufs=1))
+        psum_g = ctx.enter_context(tc.psum_pool(name="psum_g", bufs=2))
 
         w1_rows = []
         for u in range(HALVES):
@@ -122,7 +122,10 @@ def tile_blocksa_pa_t_kernel(tc, h, s2t_W1_w, s2t_W1_b, s2t_W_w, out):
 
         def group_h_token_2(b):
             dst, src = group_views(h_banks[b][1], 1, h_grouped[b][:, 2 * P : 3 * P, :])
-            nc.vector.tensor_copy(out=dst, in_=src)
+            if b % 4 != 3:
+                nc.vector.tensor_copy(out=dst, in_=src)
+            else:
+                nc.scalar.copy(out=dst, in_=src)
 
         def quantise_h(b):
             h_codes[b] = work.tile([P, TOK], U32, align_bytes=64, name="h_codes")

@@ -41,21 +41,18 @@ def tile_blocksa_pa_t_kernel(tc, h, s2t_W1_w, s2t_W1_b, s2t_W_w, out):
         ring = ctx.enter_context(tc.psum_pool(name="ring", bufs=RING_BANKS))
         psum_g = ctx.enter_context(tc.psum_pool(name="psum_g", bufs=2))
 
-        w1_rows = []
-        for u in range(HALVES):
-            half = setup.tile([P, 2, H], BF16, name="w1_rows_%d" % u)
-            nc.sync.dma_start(out=half[:], in_=s2t_W1_w[2 * u * P : 2 * (u + 1) * P].rearrange("(p e) k -> p e k", e=2))
-            w1_rows.append(half)
+        w1_rows = setup.tile([P, PACK, H], BF16)
+        nc.sync.dma_start(
+            out=w1_rows[:].rearrange("p (u e) k -> p u (e k)", u=HALVES),
+            in_=s2t_W1_w.rearrange("(u p e) k -> p u (e k)", u=HALVES, e=2),
+        )
         h_all = keep.tile([P, BATCHES, TOKENS, H], BF16)
         nc.sync.dma_start(out=h_all[:, 0], in_=h[0])
         bias_rows = setup.tile([P, H], BF16)
         nc.vector.memset(bias_rows[:], 0.0)
         nc.sync.dma_start(out=bias_rows[0:1, :], in_=s2t_W1_b.rearrange("(o k) -> o k", o=1))
-        w_rows = []
-        for a in range(HALVES):
-            half = setup.tile([P, 2, H], BF16, name="w_rows_%d" % a)
-            nc.sync.dma_start(out=half[:], in_=s2t_W_w[2 * a * P : 2 * (a + 1) * P].rearrange("(i p) k -> p i k", p=P))
-            w_rows.append(half)
+        w_rows = setup.tile([P, PACK, H], BF16)
+        nc.sync.dma_start(out=w_rows[:], in_=s2t_W_w.rearrange("(a p) k -> p a k", p=P))
         for b in range(1, BATCHES):
             nc.sync.dma_start(out=h_all[:, b], in_=h[b])
 
@@ -97,9 +94,9 @@ def tile_blocksa_pa_t_kernel(tc, h, s2t_W1_w, s2t_W1_b, s2t_W_w, out):
             grouped = setup.tile([P, H, PACK], BF16, align_bytes=64, name=name + "_grouped")
             codes = keep.tile([P, H], U32, align_bytes=64, name=name + "_codes")
             scales = keep.tile([P, H], U8, align_bytes=64, name=name + "_scales")
-            for a, half in enumerate(rows):
-                bank = transpose_rows([half[:, 0, :], half[:, 1, :]])
-                dst, src = group_views(bank, 2, grouped[:, 2 * a * P : 2 * (a + 1) * P, :])
+            for a in range(0, PACK, 2):
+                bank = transpose_rows([rows[:, a, :], rows[:, a + 1, :]])
+                dst, src = group_views(bank, 2, grouped[:, a * P : (a + 2) * P, :])
                 if a == 0:
                     nc.scalar.copy(out=dst, in_=src)
                 else:

@@ -119,10 +119,7 @@ def tile_blocksa_pa_t_kernel(tc, h, s2t_W1_w, s2t_W1_b, s2t_W_w, out):
 
         def group_h_token_2(b):
             dst, src = group_views(h_banks[b][1], 1, h_grouped[b][:, 2 * P : 3 * P, :])
-            if b % 4 != 3:
-                nc.vector.tensor_copy(out=dst, in_=src)
-            else:
-                nc.scalar.copy(out=dst, in_=src)
+            nc.vector.tensor_copy(out=dst, in_=src)
 
         def quantise_h(b):
             h_codes[b] = work.tile([P, TOK], U32, align_bytes=64, name="h_codes")

from contextlib import ExitStack

import concourse.mybir as mybir
from concourse.masks import make_identity

F32 = mybir.dt.float32
BF16 = mybir.dt.bfloat16
U32 = mybir.dt.uint32
U8 = mybir.dt.uint8
FP8X4 = mybir.dt.float8_e4m3fn_x4
ACT = mybir.ActivationFunctionType
ALU = mybir.AluOpType

P = 128
PACK = 4
HALVES = 2
BATCHES = 16
TOKENS = 3
H = 512
TOK = TOKENS * P

TOKEN_SLICES = ((0, 256), (256, 128))


RING_BANKS = 6

PE_BATCHES = (4, 8, 12)

LAG = 6

FLOPS = 2 * 2 * BATCHES * TOK * H * H


def tile_blocksa_pa_t_kernel(tc, h, s2t_W1_w, s2t_W1_b, s2t_W_w, out):
    nc = tc.nc
    with ExitStack() as ctx:
        ctx.enter_context(tc.manual_schedule(engines={mybir.EngineType.Activation}))
        keep = ctx.enter_context(tc.tile_pool(name="keep", bufs=1))
        setup = ctx.enter_context(tc.tile_pool(name="setup", bufs=1))
        work = ctx.enter_context(tc.tile_pool(name="work", bufs=2))
        ring = ctx.enter_context(tc.psum_pool(name="ring", bufs=RING_BANKS))
        psum_g = ctx.enter_context(tc.psum_pool(name="psum_g", bufs=2))

        w1_rows = setup.tile([P, PACK, H], BF16)
        nc.sync.dma_start(
            out=w1_rows[:].rearrange("p (u e) k -> p u (e k)", u=HALVES),
            in_=s2t_W1_w.rearrange("(u p e) k -> p u (e k)", u=HALVES, e=2),
        )
        h_all = keep.tile([P, BATCHES, TOKENS, H], BF16)
        nc.sync.dma_start(out=h_all[:, 0], in_=h[0])
        bias_rows = setup.tile([P, H], BF16)
        nc.vector.memset(bias_rows[:], 0.0)
        nc.sync.dma_start(out=bias_rows[0:1, :], in_=s2t_W1_b.rearrange("(o k) -> o k", o=1))
        w_rows = setup.tile([P, PACK, H], BF16)
        nc.sync.dma_start(out=w_rows[:], in_=s2t_W_w.rearrange("(a p) k -> p a k", p=P))
        for b in range(1, BATCHES):
            nc.sync.dma_start(out=h_all[:, b], in_=h[b])

        ident_f32 = keep.tile([P, P], F32)
        make_identity(nc, ident_f32[:])
        ident_bf16 = keep.tile([P, P], BF16)
        nc.vector.tensor_copy(out=ident_bf16[:], in_=ident_f32[:])
        neg_ident_bf16 = keep.tile([P, P], BF16)
        nc.vector.tensor_scalar_mul(out=neg_ident_bf16[:], in0=ident_f32[:], scalar1=-1.0)
        half_bf16 = keep.tile([P, P], BF16)
        nc.vector.tensor_scalar_mul(out=half_bf16[:], in0=ident_f32[:], scalar1=0.5)
        neg_half_bf16 = keep.tile([P, P], BF16)
        nc.vector.tensor_scalar_mul(out=neg_half_bf16[:], in0=ident_f32[:], scalar1=-0.5)

        def transpose_rows(row_tiles):
            bank = ring.tile([P, 2, HALVES, P], F32, name="bank")
            for a, rows in enumerate(row_tiles):
                words = rows.bitcast(F32)
                for u in range(HALVES):
                    nc.tensor.transpose(out=bank[:, a, u, :], in_=words[:, u * P : (u + 1) * P], identity=ident_f32[:])
            return bank

        def group_views(bank, count, grouped):
            grouped_words = grouped.rearrange("p r t -> p (r t)").bitcast(F32)
            return (
                grouped_words.rearrange("p (a r u) -> p a r u", a=count, u=HALVES),
                bank[:, 0:count].rearrange("p a u r -> p a r u"),
            )

        def quantise(grouped, codes, scales, first, count):
            cols = slice(first, first + count)
            nc.vector.quantize_mx(
                out=codes[:, cols].bitcast(FP8X4),
                scales=scales[:, cols],
                in_=grouped[:, cols, :].rearrange("p c t -> p (c t)"),
            )

        def group_weight(rows, name):
            grouped = setup.tile([P, H, PACK], BF16, align_bytes=64, name=name + "_grouped")
            codes = keep.tile([P, H], U32, align_bytes=64, name=name + "_codes")
            scales = keep.tile([P, H], U8, align_bytes=64, name=name + "_scales")
            for a in range(0, PACK, 2):
                bank = transpose_rows([rows[:, a, :], rows[:, a + 1, :]])
                dst, src = group_views(bank, 2, grouped[:, a * P : (a + 2) * P, :])
                if a == 0:
                    nc.scalar.copy(out=dst, in_=src)
                else:
                    nc.vector.tensor_copy(out=dst, in_=src)
            return grouped, codes, scales

        h_banks, h_grouped, h_codes, h_scales = {}, {}, {}, {}
        f_acc, f_planes, f_grouped, f_codes, f_scales = {}, {}, {}, {}, {}
        z_diff, h1_minus_h0, h0_minus_h2, t01, e_to_2 = {}, {}, {}, {}, {}
        share2 = keep.tile([P, BATCHES, H], F32)
        excess = keep.tile([P, BATCHES, H], F32)

        def transpose_h(b):
            h_banks[b] = (transpose_rows([h_all[:, b, 0, :], h_all[:, b, 1, :]]), transpose_rows([h_all[:, b, 2, :]]))
            h_grouped[b] = work.tile([P, TOK, PACK], BF16, align_bytes=64, name="h_grouped")

        def group_h_tokens_01(b):
            dst, src = group_views(h_banks[b][0], 2, h_grouped[b][:, 0 : 2 * P, :])
            nc.scalar.copy(out=dst, in_=src)

        def group_h_token_2(b):
            dst, src = group_views(h_banks[b][1], 1, h_grouped[b][:, 2 * P : 3 * P, :])
            nc.vector.tensor_copy(out=dst, in_=src)

        def quantise_h(b):
            h_codes[b] = work.tile([P, TOK], U32, align_bytes=64, name="h_codes")
            h_scales[b] = work.tile([P, TOK], U8, align_bytes=64, name="h_scales")
            for first, count in TOKEN_SLICES:
                quantise(h_grouped[b], h_codes[b], h_scales[b], first, count)

        def hidden_matmuls(b):
            for t in range(PACK):
                hidden = slice(t * P, (t + 1) * P)
                f_acc[b, t] = ring.tile([P, TOK], F32, name="bank")
                for first, count in TOKEN_SLICES:
                    cols = slice(first, first + count)
                    nc.tensor.matmul_mx(
                        out=f_acc[b, t][:, cols],
                        lhsT=w1_codes[:, hidden].bitcast(FP8X4),
                        lhsT_scale=w1_scales[:, hidden],
                        rhs=h_codes[b][:, cols].bitcast(FP8X4),
                        rhs_scale=h_scales[b][:, cols],
                        start=True,
                        stop=True,
                    )

        def hidden_relu(b):
            f_planes[b] = work.tile([P, PACK, TOK], BF16, name="f_planes")
            for t in range(PACK):
                nc.scalar.activation(
                    out=f_planes[b][:, t, :], in_=f_acc[b, t][:], func=ACT.Relu, bias=bias[:, t : t + 1], scale=1.0
                )

        def regroup_f(b):
            f_grouped[b] = work.tile([P, TOK, PACK], BF16, align_bytes=64, name="f_grouped")
            for first, count in TOKEN_SLICES if b == BATCHES - 1 else ((0, TOK),):
                cols = slice(first, first + count)
                nc.vector.tensor_copy(
                    out=f_grouped[b][:, cols, :].rearrange("p (c i) t -> p c t i", i=8),
                    in_=f_planes[b][:, :, cols].rearrange("p t (c i) -> p c t i", i=8),
                )

        def quantise_f(b):
            f_codes[b] = work.tile([P, TOK], U32, align_bytes=64, name="f_codes")
            f_scales[b] = work.tile([P, TOK], U8, align_bytes=64, name="f_scales")
            for first, count in TOKEN_SLICES:
                quantise(f_grouped[b], f_codes[b], f_scales[b], first, count)

        def differences(b):
            for plus, minus in ((1, 0), (0, 2), (1, 2)):
                z_diff[b, plus, minus] = ring.tile([P, H], F32, name="bank")
                for token, codes, scales in ((plus, w_codes, w_scales), (minus, neg_w_codes, neg_w_scales)):
                    tokens = slice(token * P, (token + 1) * P)
                    nc.tensor.matmul_mx(
                        out=z_diff[b, plus, minus][:],
                        lhsT=f_codes[b][:, tokens].bitcast(FP8X4),
                        lhsT_scale=f_scales[b][:, tokens],
                        rhs=codes[:].bitcast(FP8X4),
                        rhs_scale=scales[:],
                        start=(token == plus),
                        stop=(token == minus),
                    )
            h1_minus_h0[b] = psum_g.tile([P, H], F32, name="h1_minus_h0")
            nc.tensor.matmul(out=h1_minus_h0[b][:], lhsT=half_bf16[:], rhs=h_all[:, b, 1, :], start=True, stop=False)
            nc.tensor.matmul(out=h1_minus_h0[b][:], lhsT=neg_half_bf16[:], rhs=h_all[:, b, 0, :], start=False, stop=True)

        def tanh_and_exps(b):
            t01[b] = work.tile([P, H], F32, name="t01")
            nc.scalar.activation(out=t01[b][:], in_=z_diff[b, 1, 0][:], func=ACT.Tanh, scale=0.5)
            e_to_2[b] = work.tile([P, 2, H], F32, name="e_to_2")
            for token in range(2):
                nc.scalar.activation(out=e_to_2[b][:, token, :], in_=z_diff[b, token, 2][:], func=ACT.Exp)

        def sum_and_product(b):
            nc.vector.tensor_tensor(out=share2[:, b, :], in0=e_to_2[b][:, 0, :], in1=e_to_2[b][:, 1, :], op=ALU.add)
            nc.vector.scalar_tensor_tensor(
                out=excess[:, b, :], in0=t01[b][:], scalar=1.0, in1=h1_minus_h0[b][:], op0=ALU.add, op1=ALU.mult
            )

        def token_0_minus_2(b):
            h0_minus_h2[b] = psum_g.tile([P, H], F32, name="h1_minus_h0")
            nc.tensor.matmul(out=h0_minus_h2[b][:], lhsT=ident_bf16[:], rhs=h_all[:, b, 0, :], start=True, stop=False)
            nc.tensor.matmul(out=h0_minus_h2[b][:], lhsT=neg_ident_bf16[:], rhs=h_all[:, b, 2, :], start=False, stop=True)

        def add_token_0(b):
            if b in PE_BATCHES:
                token_0_minus_2(b)
                nc.vector.tensor_tensor(out=excess[:, b, :], in0=excess[:, b, :], in1=h0_minus_h2[b][:], op=ALU.add)
            else:
                nc.vector.tensor_tensor(out=excess[:, b, :], in0=excess[:, b, :], in1=h_all[:, b, 0, :], op=ALU.add)

        def subtract_token_2(b):
            if b not in PE_BATCHES:
                nc.vector.tensor_tensor(out=excess[:, b, :], in0=excess[:, b, :], in1=h_all[:, b, 2, :], op=ALU.subtract)

        def root_of_share_2(b, cols):
            nc.scalar.activation(
                out=share2[:, b, cols], in_=share2[:, b, cols], func=ACT.Abs_reciprocal_sqrt, bias=1.0, scale=1.0
            )

        def share_of_token_2(b, cols):
            nc.scalar.activation(out=share2[:, b, cols], in_=share2[:, b, cols], func=ACT.Square)

        def weigh_excess(b, cols):
            nc.vector.scalar_tensor_tensor(
                out=excess[:, b, cols],
                in0=share2[:, b, cols],
                scalar=-1.0,
                in1=excess[:, b, cols],
                op0=ALU.add,
                op1=ALU.mult,
            )

        def subtract_and_store(b, cols):
            nc.vector.tensor_tensor(out=excess[:, b, cols], in0=h_all[:, b, 2, cols], in1=excess[:, b, cols], op=ALU.subtract)
            nc.sync.dma_start(out=out[b, :, cols], in_=excess[:, b, cols])

        def live(b):
            return 0 <= b < BATCHES

        w1_grouped, w1_codes, w1_scales = group_weight(w1_rows, "w1")
        transpose_h(0)
        group_h_tokens_01(0)
        for a in range(HALVES):
            quantise(w1_grouped, w1_codes, w1_scales, 2 * a * P, 2 * P)
        group_h_token_2(0)

        bias_words = transpose_rows([bias_rows[:]])
        bias_grouped = setup.tile([P, PACK], BF16)
        nc.scalar.copy(out=bias_grouped[:].bitcast(F32), in_=bias_words[:, 0, :, 0])
        bias = keep.tile([P, PACK], F32)
        nc.vector.tensor_copy(out=bias[:], in_=bias_grouped[:])

        quantise_h(0)
        w_grouped, w_codes, w_scales = group_weight(w_rows, "w")
        transpose_h(1)
        hidden_matmuls(0)
        quantise(w_grouped, w_codes, w_scales, 0, H)
        neg_w_grouped = setup.tile([P, H, PACK], BF16, align_bytes=64)
        nc.vector.tensor_scalar_mul(out=neg_w_grouped[:], in0=w_grouped[:], scalar1=-1.0)
        neg_w_codes = keep.tile([P, H], U32, align_bytes=64)
        neg_w_scales = keep.tile([P, H], U8, align_bytes=64)
        quantise(neg_w_grouped, neg_w_codes, neg_w_scales, 0, H)

        for i in range(BATCHES + 2):
            if live(i + 1):
                group_h_tokens_01(i + 1)
                group_h_token_2(i + 1)
            if live(i - 2):
                sum_and_product(i - 2)
            if live(i - 1):
                differences(i - 1)
            if live(i + 1):
                quantise_h(i + 1)
            if live(i):
                hidden_relu(i)
            if live(i + 2):
                transpose_h(i + 2)
            if live(i):
                regroup_f(i)
            if live(i - 1):
                tanh_and_exps(i - 1)
            if live(i + 1):
                hidden_matmuls(i + 1)
            if live(i - 2):
                add_token_0(i - 2)
            if live(i):
                quantise_f(i)
            if live(i - 2 - LAG):
                subtract_token_2(i - 2 - LAG)
        for b in range(BATCHES - LAG, BATCHES):
            subtract_token_2(b)

        pieces = []
        for b in range(BATCHES):
            count = 2 if b in (0, BATCHES - 1) else 1
            for part in range(count):
                pieces.append((b, slice(part * H // count, (part + 1) * H // count)))
        for i in range(len(pieces) + 2):
            if i < len(pieces):
                root_of_share_2(*pieces[i])
            if 1 <= i <= len(pieces):
                share_of_token_2(*pieces[i - 1])
                weigh_excess(*pieces[i - 1])
            if i >= 2:
                subtract_and_store(*pieces[i - 2])
